import numpy as np
import ml_dtypes


def mxq(x, axis, fmt="e4m3"):
    dtype, down = {"e4m3": (ml_dtypes.float8_e4m3fn, 7), "e5m2": (ml_dtypes.float8_e5m2, 14)}[fmt]
    v = np.moveaxis(np.asarray(x, np.float32).astype(ml_dtypes.bfloat16).astype(np.float64), axis, -1)
    blocks = v.reshape(v.shape[:-1] + (-1, 32))
    amax = np.abs(blocks).max(-1, keepdims=True)
    byte = np.maximum(np.where(amax > 0, np.frexp(amax)[1] - 1 + 127, 0) - down, 1)
    scale = np.exp2(byte - 127.0)
    codes = (blocks / scale).astype(np.float32).astype(dtype).astype(np.float64)
    return np.moveaxis((codes * scale).reshape(v.shape), -1, axis)


WIDE = False


def mx_kscale(k):
    if not WIDE:
        return np.ones(k)
    levels = np.array([10, -10, 5, -5, 0])
    if k % 512:
        return np.exp2(np.random.permutation(np.resize(levels, k // 32))).repeat(32)
    a = np.empty((k // 512, 16))
    for p in range(k // 512):
        a[p, :8] = np.random.permutation(np.resize(levels, 8))
        for g in range(8):
            far = levels[np.abs(levels - a[p, g]) >= 10]
            a[p, g + 8] = far[np.random.randint(len(far))]
    return np.exp2(a.ravel()).repeat(32)


BF16 = ml_dtypes.bfloat16


def bf(x):
    return np.asarray(x, np.float32).astype(BF16)


def f64(x):
    return np.asarray(x).astype(np.float64)


N, K, D_IN, HC, H = 4096, 4, 512, 512, 256


def sigmoid(v):
    return 1.0 / (1.0 + np.exp(-v))


def setup_inputs():
    s, t = mx_kscale(D_IN), mx_kscale(HC)
    d = {
        "x": bf(np.random.standard_normal((N, D_IN)) * s),
        "child_h": bf(np.random.standard_normal((N, K, HC)) * t),
        "fc_sum": bf(np.random.standard_normal((N, H)) * 0.27 * np.sqrt(K)),
    }
    for g in ("i", "o", "u"):
        d["W" + g] = bf(np.random.standard_normal((D_IN, H)) * 0.7 / np.sqrt(D_IN) / s[:, None])
        d["bW" + g] = bf(np.random.standard_normal(H) * 0.3)
        d["U" + g] = bf(np.random.standard_normal((HC, H)) * 0.7 / np.sqrt(K * HC) / t[:, None])
        d["bU" + g] = bf(np.random.standard_normal(H) * 0.3)
    return d


def reference(x, child_h, fc_sum, Wi, bWi, Ui, bUi, Wo, bWo, Uo, bUo, Wu, bWu, Uu, bUu):
    h_sum = f64(child_h).sum(axis=1)
    xq = mxq(f64(x), 1, "e4m3")
    hq = mxq(h_sum, 1, "e4m3")
    i = sigmoid((xq @ mxq(f64(Wi), 0, "e4m3")) + f64(bWi) + (hq @ mxq(f64(Ui), 0, "e4m3")) + f64(bUi))
    o = sigmoid((xq @ mxq(f64(Wo), 0, "e4m3")) + f64(bWo) + (hq @ mxq(f64(Uo), 0, "e4m3")) + f64(bUo))
    u = np.tanh((xq @ mxq(f64(Wu), 0, "e4m3")) + f64(bWu) + (hq @ mxq(f64(Uu), 0, "e4m3")) + f64(bUu))
    c = i * u + f64(fc_sum)
    h = o * np.tanh(c)
    return np.stack([h, c], axis=0)

@@ -1,0 +1,296 @@
+from contextlib import ExitStack
+
+import concourse.mybir as mybir
+from concourse.masks import make_identity
+
+F32 = mybir.dt.float32
+BF16 = mybir.dt.bfloat16
+U32 = mybir.dt.uint32
+U8 = mybir.dt.uint8
+FP8X4 = mybir.dt.float8_e4m3fn_x4
+ACT = mybir.ActivationFunctionType
+ALU = mybir.AluOpType
+
+P = 128
+PACK = 4
+NODES, CHILDREN, D, H = 4096, 4, 512, 256
+GATES = 3
+
+SLOTS = 2
+STEPS = NODES // (P * SLOTS)
+GROUP_NODES = P // CHILDREN
+BANK_GROUPS = 4
+PG = GROUP_NODES // SLOTS
+PB = PG * BANK_GROUPS
+LOAD_AHEAD = 6
+FC_LATER = 3
+STORE_LAG = STEPS - LOAD_AHEAD - 3 + FC_LATER
+
+FLOPS = 2 * NODES * D * H * 2 * GATES
+
+
+def tile_childsumtreelstmcell_pb_t_kernel(
+    tc, x, child_h, fc_sum, Wi, bWi, Ui, bUi, Wo, bWo, Uo, bUo, Wu, bWu, Uu, bUu, out
+):
+    nc = tc.nc
+    with ExitStack() as ctx:
+        ctx.enter_context(tc.manual_schedule())
+        const = ctx.enter_context(tc.tile_pool(name="const", bufs=1))
+        loads = ctx.enter_context(tc.tile_pool(name="loads", bufs=LOAD_AHEAD))
+        sides = ctx.enter_context(tc.tile_pool(name="sides", bufs=2))
+        work = ctx.enter_context(tc.tile_pool(name="work", bufs=2))
+        psum = ctx.enter_context(tc.psum_pool(name="psum", bufs=1))
+
+        x_view = x.rearrange("(s p j) d -> s p (j d)", p=P, j=SLOTS)
+        fc_view = fc_sum.rearrange("(s p j) d -> s p (j d)", p=P, j=SLOTS)
+        out_view = out.rearrange("o (s p j) d -> s p o (j d)", p=P, j=SLOTS)
+        ch_view = child_h.rearrange("n k d -> (n k) d").rearrange(
+            "(b g q) d -> b q g d", g=BANK_GROUPS, q=P
+        )
+
+        x_sb, fc_sb, ch_sb, hT_ps, xT_ps = {}, {}, {}, {}, {}
+        x_side, h_side, x_q, h_q, io_ps, u_ps = {}, {}, {}, {}, {}, {}
+        pre, tanh_c, out_sb = {}, {}, {}
+
+        def live(s):
+            return 0 <= s < STEPS
+
+        def load(s):
+            if not live(s):
+                return
+            for b in range(SLOTS):
+                ch_sb[s, b] = loads.tile(
+                    [P, BANK_GROUPS, D], BF16, tag="ch", bufs=SLOTS * LOAD_AHEAD, name="ch_sb"
+                )
+                nc.sync.dma_start(out=ch_sb[s, b][:], in_=ch_view[SLOTS * s + b])
+            x_sb[s] = loads.tile([P, SLOTS * D], BF16, tag="x", name="x_sb")
+            nc.sync.dma_start(out=x_sb[s][:], in_=x_view[s])
+
+        def load_fc(s):
+            if not live(s):
+                return
+            fc_sb[s] = loads.tile([P, SLOTS, H], BF16, tag="fc", name="fc_sb")
+            nc.sync.dma_start(out=fc_sb[s][:].rearrange("p j d -> p (j d)"), in_=fc_view[s])
+
+        load(0)
+
+        w_raw = const.tile([P, GATES, PACK, H], BF16)
+        u_raw = const.tile([P, GATES, PACK, H], BF16)
+        for g, (w_mat, u_mat) in enumerate(((Wi, Ui), (Wo, Uo), (Wu, Uu))):
+            nc.sync.dma_start(out=w_raw[:, g], in_=w_mat.rearrange("(w t) c -> w t c", t=PACK))
+            nc.sync.dma_start(out=u_raw[:, g], in_=u_mat.rearrange("(w t) c -> w t c", t=PACK))
+        w_side = const.tile([P, GATES, H, PACK], BF16, align_bytes=64)
+        u_side = const.tile([P, GATES, H, PACK], BF16, align_bytes=64)
+        w_codes = const.tile([P, GATES * H], U32, align_bytes=64)
+        u_codes = const.tile([P, GATES * H], U32, align_bytes=64)
+        w_scales = const.tile([P, GATES * H], U8, align_bytes=64)
+        u_scales = const.tile([P, GATES * H], U8, align_bytes=64)
+
+        def quantise_weights():
+            for g in range(GATES):
+                cols = slice(H * g, H * (g + 1))
+                nc.vector.tensor_copy(out=w_side[:, g], in_=w_raw[:, g].rearrange("w t c -> w c t"))
+                nc.scalar.copy(out=u_side[:, g], in_=u_raw[:, g].rearrange("w t c -> w c t"))
+                for side, codes, scales in ((w_side, w_codes, w_scales), (u_side, u_codes, u_scales)):
+                    nc.vector.quantize_mx(
+                        out=codes[:, cols].bitcast(FP8X4),
+                        scales=scales[:, cols],
+                        in_=side[:, g].rearrange("w c t -> w (c t)"),
+                    )
+
+        ident = const.tile([P, P], F32)
+        make_identity(nc, ident[:])
+        bias_rows = const.tile([P, GATES * H], BF16)
+        nc.vector.memset(bias_rows[:], 0.0)
+        for g, (b_w, b_u) in enumerate(((bWi, bUi), (bWo, bUo), (bWu, bUu))):
+            cols = slice(H * g, H * (g + 1))
+            nc.gpsimd.dma_start(out=bias_rows[0:1, cols], in_=b_w.rearrange("(o h) -> o h", o=1))
+            nc.gpsimd.dma_start(out=bias_rows[1:2, cols], in_=b_u.rearrange("(o h) -> o h", o=1))
+        ones = const.tile([P, P], BF16)
+        nc.vector.memset(ones[:], 1.0)
+        warm = const.tile([P, 1], F32)
+        nc.vector.memset(warm[:], 0.0)
+        nc.scalar.activation(out=warm[:], in_=warm[:], func=ACT.Sigmoid)
+        sel_nat = const.tile([P, GROUP_NODES], F32)
+        nc.vector.tensor_reduce(
+            out=sel_nat[:],
+            in_=ident[:].rearrange("q (n k) -> q n k", k=CHILDREN),
+            axis=mybir.AxisListType.X,
+            op=ALU.add,
+        )
+        sel = const.tile([P, SLOTS, PG], BF16)
+        nc.vector.tensor_copy(out=sel[:], in_=sel_nat[:].rearrange("q (a j) -> q j a", j=SLOTS))
+
+        bias = const.tile([P, GATES * H], F32)
+
+        def build_bias():
+            bias_io_ps = psum.tile([P, 2 * H], F32, tag="io", bufs=2)
+            nc.tensor.matmul(
+                out=bias_io_ps[:], lhsT=ones[:], rhs=bias_rows[:, 0 : 2 * H], start=True, stop=True
+            )
+            nc.vector.tensor_copy(out=bias[:, 0 : 2 * H], in_=bias_io_ps[:])
+            bias_u_ps = psum.tile([P, SLOTS, H], F32, tag="u", bufs=1)
+            nc.tensor.matmul(
+                out=bias_u_ps[:, 0, :],
+                lhsT=ones[:],
+                rhs=bias_rows[:, 2 * H : 3 * H],
+                start=True,
+                stop=True,
+            )
+            nc.vector.tensor_copy(out=bias[:, 2 * H : 3 * H], in_=bias_u_ps[:, 0, :])
+
+        def sum_children(s):
+            if not live(s):
+                return
+            for b in range(SLOTS):
+                hT_ps[s, b] = psum.tile([P, SLOTS, PACK, PB], F32, tag="hT", bufs=2 * SLOTS, name="hT_ps")
+                for g in range(BANK_GROUPS):
+                    for t in range(PACK):
+                        nc.tensor.matmul(
+                            out=hT_ps[s, b][:, :, t, PG * g : PG * (g + 1)],
+                            lhsT=ch_sb[s, b][:, g, t:D:PACK],
+                            rhs=sel[:],
+                            start=True,
+                            stop=True,
+                        )
+
+        def round_h(s):
+            if not live(s):
+                return
+            h_side[s] = sides.tile([P, SLOTS * P * PACK], BF16, align_bytes=64, tag="h_side", name="h_side")
+            view = h_side[s][:].rearrange("w (j p t) -> w j p t", j=SLOTS, t=PACK)
+            for b in range(SLOTS):
+                nc.scalar.copy(
+                    out=view[:, :, PB * b : PB * (b + 1), :],
+                    in_=hT_ps[s, b][:].rearrange("w j t p -> w j p t"),
+                )
+
+        def transpose_x(s):
+            if not live(s):
+                return
+            xT_ps[s] = psum.tile([P, SLOTS, 2, P], F32, tag="xT", bufs=1, name="xT_ps")
+            words = x_sb[s][:].bitcast(F32)
+            for j in range(SLOTS):
+                for u in range(2):
+                    every_2nd = slice((D // 2) * j + u, (D // 2) * (j + 1), 2)
+                    nc.tensor.transpose(xT_ps[s][:, j, u, :], words[:, every_2nd], ident[:])
+
+        def copy_x(s):
+            if not live(s):
+                return
+            x_side[s] = sides.tile([P, SLOTS * P * PACK], BF16, align_bytes=64, tag="x_side", name="x_side")
+            nc.vector.tensor_copy(
+                out=x_side[s][:].bitcast(F32).rearrange("w (j p u) -> w j p u", j=SLOTS, u=2),
+                in_=xT_ps[s][:].rearrange("w j u p -> w j p u"),
+            )
+
+        def quantise(s, side, quantised, name):
+            if not live(s):
+                return
+            codes = sides.tile([P, SLOTS * P], U32, align_bytes=64, tag=name + "_codes", name=name + "_codes")
+            scales = sides.tile([P, SLOTS * P], U8, align_bytes=64, tag=name + "_scales", name=name + "_scales")
+            nc.vector.quantize_mx(out=codes[:].bitcast(FP8X4), scales=scales[:], in_=side[s][:])
+            quantised[s] = (codes, scales)
+
+        def multiply(s):
+            if not live(s):
+                return
+            for j in range(SLOTS):
+                io_ps[s, j] = psum.tile([P, 2 * H], F32, tag="io", bufs=2, name="io_ps")
+            u_ps[s] = psum.tile([P, SLOTS, H], F32, tag="u", bufs=1, name="u_ps")
+            groups = [(io_ps[s, j][:], j, slice(0, 2 * H)) for j in range(SLOTS)]
+            groups += [(u_ps[s][:, j, :], j, slice(2 * H, 3 * H)) for j in range(SLOTS)]
+            for acc, j, cols in groups:
+                nodes = slice(P * j, P * (j + 1))
+                for part, (a_q, b_codes, b_scales) in enumerate(
+                    ((x_q[s], w_codes, w_scales), (h_q[s], u_codes, u_scales))
+                ):
+                    nc.tensor.matmul_mx(
+                        out=acc,
+                        lhsT=a_q[0][:, nodes].bitcast(FP8X4),
+                        lhsT_scale=a_q[1][:, nodes],
+                        rhs=b_codes[:, cols].bitcast(FP8X4),
+                        rhs_scale=b_scales[:, cols],
+                        start=(part == 0),
+                        stop=(part == 1),
+                    )
+
+        def add_bias_io(s, j):
+            if not live(s):
+                return
+            if j == 0:
+                pre[s] = work.tile([P, SLOTS, GATES * H], F32, tag="pre", bufs=4, name="pre")
+            nc.vector.tensor_tensor(
+                out=pre[s][:, j, 0 : 2 * H], in0=io_ps[s, j][:], in1=bias[:, 0 : 2 * H], op=ALU.add
+            )
+
+        def add_bias_u(s):
+            if not live(s):
+                return
+            nc.vector.tensor_tensor(
+                out=pre[s][:, :, 2 * H : 3 * H],
+                in0=u_ps[s][:],
+                in1=bias[:, 2 * H : 3 * H].unsqueeze(1).to_broadcast([P, SLOTS, H]),
+                op=ALU.add,
+            )
+
+        def activate(s):
+            if not live(s):
+                return
+            for lo, func in ((0, ACT.Sigmoid), (2 * H, ACT.Tanh), (H, ACT.Sigmoid)):
+                gate = pre[s][:, :, lo : lo + H]
+                nc.scalar.activation(out=gate, in_=gate, func=func)
+
+        def cell(s):
+            if not live(s):
+                return
+            out_sb[s] = work.tile([P, 2, SLOTS, H], F32, tag="out", bufs=STORE_LAG + 4, name="out_sb")
+            c_new = out_sb[s][:, 1]
+            nc.gpsimd.tensor_tensor(
+                out=c_new, in0=pre[s][:, :, 0:H], in1=pre[s][:, :, 2 * H : 3 * H], op=ALU.mult
+            )
+            nc.gpsimd.tensor_tensor(out=c_new, in0=c_new, in1=fc_sb[s][:], op=ALU.add)
+
+        def tanh_cell(s):
+            if not live(s):
+                return
+            tanh_c[s] = work.tile([P, SLOTS, H], F32, tag="tanh_c", name="tanh_c")
+            nc.scalar.activation(out=tanh_c[s][:], in_=out_sb[s][:, 1], func=ACT.Tanh)
+
+        def hidden(s):
+            if not live(s):
+                return
+            nc.vector.tensor_tensor(
+                out=out_sb[s][:, 0], in0=pre[s][:, :, H : 2 * H], in1=tanh_c[s][:], op=ALU.mult
+            )
+
+        def store(s):
+            if not live(s):
+                return
+            nc.sync.dma_start(out=out_view[s], in_=out_sb[s][:].rearrange("p o j d -> p o (j d)"))
+
+        def iteration(t):
+            load(t + LOAD_AHEAD)
+            load_fc(t + LOAD_AHEAD - FC_LATER)
+            store(t - 3 - STORE_LAG)
+            multiply(t)
+            hidden(t - 3)
+            copy_x(t + 1)
+            add_bias_io(t, 0)
+            round_h(t + 1)
+            quantise(t + 1, h_side, h_q, "h")
+            quantise(t + 1, x_side, x_q, "x")
+            add_bias_io(t, 1)
+            add_bias_u(t)
+            sum_children(t + 2)
+            transpose_x(t + 2)
+            activate(t - 1)
+            cell(t - 1)
+            tanh_cell(t - 2)
+
+        for t in range(1 - LOAD_AHEAD, 0):
+            iteration(t)
+        quantise_weights()
+        build_bias()
+        for t in range(0, STEPS + 3 + STORE_LAG + 1):
+            iteration(t)

@@ -72,13 +72,8 @@ def tile_childsumtreelstmcell_pb_t_kernel(
             fc_sb[s] = loads.tile([P, SLOTS, H], BF16, tag="fc", name="fc_sb")
             nc.sync.dma_start(out=fc_sb[s][:].rearrange("p j d -> p (j d)"), in_=fc_view[s])
 
-        load(0)
-
         w_raw = const.tile([P, GATES, PACK, H], BF16)
         u_raw = const.tile([P, GATES, PACK, H], BF16)
-        for g, (w_mat, u_mat) in enumerate(((Wi, Ui), (Wo, Uo), (Wu, Uu))):
-            nc.sync.dma_start(out=w_raw[:, g], in_=w_mat.rearrange("(w t) c -> w t c", t=PACK))
-            nc.sync.dma_start(out=u_raw[:, g], in_=u_mat.rearrange("(w t) c -> w t c", t=PACK))
         w_side = const.tile([P, GATES, H, PACK], BF16, align_bytes=64)
         u_side = const.tile([P, GATES, H, PACK], BF16, align_bytes=64)
         w_codes = const.tile([P, GATES * H], U32, align_bytes=64)
@@ -86,26 +81,29 @@ def tile_childsumtreelstmcell_pb_t_kernel(
         w_scales = const.tile([P, GATES * H], U8, align_bytes=64)
         u_scales = const.tile([P, GATES * H], U8, align_bytes=64)
 
-        def quantise_weights():
-            for g in range(GATES):
-                cols = slice(H * g, H * (g + 1))
-                nc.vector.tensor_copy(out=w_side[:, g], in_=w_raw[:, g].rearrange("w t c -> w c t"))
-                nc.scalar.copy(out=u_side[:, g], in_=u_raw[:, g].rearrange("w t c -> w c t"))
-                for side, codes, scales in ((w_side, w_codes, w_scales), (u_side, u_codes, u_scales)):
-                    nc.vector.quantize_mx(
-                        out=codes[:, cols].bitcast(FP8X4),
-                        scales=scales[:, cols],
-                        in_=side[:, g].rearrange("w c t -> w (c t)"),
-                    )
+        def load_gate(g):
+            for raw, mat in ((w_raw, (Wi, Wo, Wu)[g]), (u_raw, (Ui, Uo, Uu)[g])):
+                nc.sync.dma_start(out=raw[:, g], in_=mat.rearrange("(w t) c -> w t c", t=PACK))
 
-        ident = const.tile([P, P], F32)
-        make_identity(nc, ident[:])
+        def arrange_w(g):
+            nc.vector.tensor_copy(out=w_side[:, g], in_=w_raw[:, g].rearrange("w t c -> w c t"))
+
+        def arrange_u(g):
+            nc.scalar.copy(out=u_side[:, g], in_=u_raw[:, g].rearrange("w t c -> w c t"))
+
+        def quantise_gate(g):
+            cols = slice(H * g, H * (g + 1))
+            for side, codes, scales in ((w_side, w_codes, w_scales), (u_side, u_codes, u_scales)):
+                nc.vector.quantize_mx(
+                    out=codes[:, cols].bitcast(FP8X4),
+                    scales=scales[:, cols],
+                    in_=side[:, g].rearrange("w c t -> w (c t)"),
+                )
+
         bias_rows = const.tile([P, GATES * H], BF16)
         nc.vector.memset(bias_rows[:], 0.0)
-        for g, (b_w, b_u) in enumerate(((bWi, bUi), (bWo, bUo), (bWu, bUu))):
-            cols = slice(H * g, H * (g + 1))
-            nc.gpsimd.dma_start(out=bias_rows[0:1, cols], in_=b_w.rearrange("(o h) -> o h", o=1))
-            nc.gpsimd.dma_start(out=bias_rows[1:2, cols], in_=b_u.rearrange("(o h) -> o h", o=1))
+        ident = const.tile([P, P], F32)
+        make_identity(nc, ident[:])
         ones = const.tile([P, P], BF16)
         nc.vector.memset(ones[:], 1.0)
         warm = const.tile([P, 1], F32)
@@ -123,12 +121,20 @@ def tile_childsumtreelstmcell_pb_t_kernel(
 
         bias = const.tile([P, GATES * H], F32)
 
+        def load_bias():
+            for g, (b_w, b_u) in enumerate(((bWi, bUi), (bWo, bUo), (bWu, bUu))):
+                cols = slice(H * g, H * (g + 1))
+                for row, vec in enumerate((b_w, b_u)):
+                    nc.sync.dma_start(
+                        out=bias_rows[row : row + 1, cols], in_=vec.rearrange("(o h) -> o h", o=1)
+                    )
+
         def build_bias():
             bias_io_ps = psum.tile([P, 2 * H], F32, tag="io", bufs=2)
             nc.tensor.matmul(
                 out=bias_io_ps[:], lhsT=ones[:], rhs=bias_rows[:, 0 : 2 * H], start=True, stop=True
             )
-            nc.vector.tensor_copy(out=bias[:, 0 : 2 * H], in_=bias_io_ps[:])
+            nc.scalar.copy(out=bias[:, 0 : 2 * H], in_=bias_io_ps[:])
             bias_u_ps = psum.tile([P, SLOTS, H], F32, tag="u", bufs=1)
             nc.tensor.matmul(
                 out=bias_u_ps[:, 0, :],
@@ -137,7 +143,7 @@ def tile_childsumtreelstmcell_pb_t_kernel(
                 start=True,
                 stop=True,
             )
-            nc.vector.tensor_copy(out=bias[:, 2 * H : 3 * H], in_=bias_u_ps[:, 0, :])
+            nc.scalar.copy(out=bias[:, 2 * H : 3 * H], in_=bias_u_ps[:, 0, :])
 
         def sum_children(s):
             if not live(s):
@@ -241,15 +247,39 @@ def tile_childsumtreelstmcell_pb_t_kernel(
                 gate = pre[s][:, :, lo : lo + H]
                 nc.scalar.activation(out=gate, in_=gate, func=func)
 
+        def new_out(s):
+            out_sb[s] = work.tile([P, 2, SLOTS, H], F32, tag="out", bufs=STORE_LAG + 4, name="out_sb")
+
         def cell(s):
             if not live(s):
                 return
-            out_sb[s] = work.tile([P, 2, SLOTS, H], F32, tag="out", bufs=STORE_LAG + 4, name="out_sb")
+            new_out(s)
             c_new = out_sb[s][:, 1]
             nc.gpsimd.tensor_tensor(
                 out=c_new, in0=pre[s][:, :, 0:H], in1=pre[s][:, :, 2 * H : 3 * H], op=ALU.mult
             )
             nc.gpsimd.tensor_tensor(out=c_new, in0=c_new, in1=fc_sb[s][:], op=ALU.add)
+
+        def cell_last():
+            s = STEPS - 1
+            new_out(s)
+            c_new = out_sb[s][:, 1]
+            for j in range(SLOTS):
+                nc.vector.tensor_tensor(
+                    out=c_new[:, j], in0=pre[s][:, j, 0:H], in1=pre[s][:, j, 2 * H : 3 * H], op=ALU.mult
+                )
+            for j in range(SLOTS):
+                nc.vector.tensor_tensor(out=c_new[:, j], in0=c_new[:, j], in1=fc_sb[s][:, j], op=ALU.add)
+
+        def finish_last():
+            s = STEPS - 1
+            tanh_c[s] = work.tile([P, SLOTS, H], F32, tag="tanh_c", name="tanh_c")
+            for j in range(SLOTS):
+                nc.scalar.activation(out=tanh_c[s][:, j], in_=out_sb[s][:, 1, j], func=ACT.Tanh)
+            for j in range(SLOTS):
+                nc.vector.tensor_tensor(
+                    out=out_sb[s][:, 0, j], in0=pre[s][:, j, H : 2 * H], in1=tanh_c[s][:, j], op=ALU.mult
+                )
 
         def tanh_cell(s):
             if not live(s):
@@ -288,9 +318,51 @@ def tile_childsumtreelstmcell_pb_t_kernel(
             cell(t - 1)
             tanh_cell(t - 2)
 
+        load_gate(0)
+        load_gate(1)
+        load(0)
+        load_bias()
+        load_gate(2)
         for t in range(1 - LOAD_AHEAD, 0):
-            iteration(t)
-        quantise_weights()
+            load(t + LOAD_AHEAD)
+            load_fc(t + LOAD_AHEAD - FC_LATER)
+        arrange_w(0)
+        arrange_u(0)
+        arrange_w(1)
+        arrange_u(1)
+        quantise_gate(0)
+        quantise_gate(1)
+        sum_children(0)
+        transpose_x(0)
+        round_h(0)
+        copy_x(0)
+        arrange_w(2)
+        arrange_u(2)
+        quantise(0, h_side, h_q, "h")
+        quantise(0, x_side, x_q, "x")
+        quantise_gate(2)
         build_bias()
-        for t in range(0, STEPS + 3 + STORE_LAG + 1):
+        load(LOAD_AHEAD)
+        load_fc(LOAD_AHEAD - FC_LATER)
+        multiply(0)
+        sum_children(1)
+        transpose_x(1)
+        add_bias_io(0, 0)
+        add_bias_io(0, 1)
+        add_bias_u(0)
+        round_h(1)
+        copy_x(1)
+        sum_children(2)
+        transpose_x(2)
+        quantise(1, h_side, h_q, "h")
+        quantise(1, x_side, x_q, "x")
+        for t in range(1, STEPS):
             iteration(t)
+        hidden(STEPS - 3)
+        activate(STEPS - 1)
+        tanh_cell(STEPS - 2)
+        cell_last()
+        hidden(STEPS - 2)
+        finish_last()
+        for s in range(STEPS - 3 - STORE_LAG, STEPS):
+            store(s)

@@ -125,25 +125,23 @@ def tile_childsumtreelstmcell_pb_t_kernel(
             for g, (b_w, b_u) in enumerate(((bWi, bUi), (bWo, bUo), (bWu, bUu))):
                 cols = slice(H * g, H * (g + 1))
                 for row, vec in enumerate((b_w, b_u)):
-                    nc.sync.dma_start(
+                    nc.gpsimd.dma_start(
                         out=bias_rows[row : row + 1, cols], in_=vec.rearrange("(o h) -> o h", o=1)
                     )
 
         def build_bias():
-            bias_io_ps = psum.tile([P, 2 * H], F32, tag="io", bufs=2)
+            bias_io_ps = psum.tile([P, 2 * H], F32, tag="hT", bufs=2 * SLOTS)
             nc.tensor.matmul(
                 out=bias_io_ps[:], lhsT=ones[:], rhs=bias_rows[:, 0 : 2 * H], start=True, stop=True
             )
             nc.scalar.copy(out=bias[:, 0 : 2 * H], in_=bias_io_ps[:])
-            bias_u_ps = psum.tile([P, SLOTS, H], F32, tag="u", bufs=1)
+            bias_u_ps = psum.tile([P, H], F32, tag="hT", bufs=2 * SLOTS)
             nc.tensor.matmul(
-                out=bias_u_ps[:, 0, :],
-                lhsT=ones[:],
-                rhs=bias_rows[:, 2 * H : 3 * H],
-                start=True,
-                stop=True,
+                out=bias_u_ps[:], lhsT=ones[:], rhs=bias_rows[:, 2 * H : 3 * H], start=True, stop=True
             )
-            nc.scalar.copy(out=bias[:, 2 * H : 3 * H], in_=bias_u_ps[:, 0, :])
+            nc.scalar.copy(out=bias[:, 2 * H : 3 * H], in_=bias_u_ps[:])
+
+        load_bias()
 
         def sum_children(s):
             if not live(s):
@@ -321,7 +319,6 @@ def tile_childsumtreelstmcell_pb_t_kernel(
         load_gate(0)
         load_gate(1)
         load(0)
-        load_bias()
         load_gate(2)
         for t in range(1 - LOAD_AHEAD, 0):
             load(t + LOAD_AHEAD)
@@ -341,12 +338,12 @@ def tile_childsumtreelstmcell_pb_t_kernel(
         quantise(0, h_side, h_q, "h")
         quantise(0, x_side, x_q, "x")
         quantise_gate(2)
-        build_bias()
         load(LOAD_AHEAD)
         load_fc(LOAD_AHEAD - FC_LATER)
         multiply(0)
         sum_children(1)
         transpose_x(1)
+        build_bias()
         add_bias_io(0, 0)
         add_bias_io(0, 1)
         add_bias_u(0)

@@ -24,6 +24,9 @@ PG = GROUP_NODES // SLOTS
 PB = PG * BANK_GROUPS
 LOAD_AHEAD = 6
 FC_LATER = 3
+X_STEPS = 2
+FC_STEPS = 4
+WIDE_STEPS = (14, 15)
 STORE_LAG = STEPS - LOAD_AHEAD - 3 + FC_LATER
 
 FLOPS = 2 * NODES * D * H * 2 * GATES
@@ -41,12 +44,12 @@ def tile_childsumtreelstmcell_pb_t_kernel(
         work = ctx.enter_context(tc.tile_pool(name="work", bufs=2))
         psum = ctx.enter_context(tc.psum_pool(name="psum", bufs=1))
 
-        x_view = x.rearrange("(s p j) d -> s p (j d)", p=P, j=SLOTS)
-        fc_view = fc_sum.rearrange("(s p j) d -> s p (j d)", p=P, j=SLOTS)
+        x_view = x.rearrange("(b i p j) d -> b p i (j d)", i=X_STEPS, p=P, j=SLOTS)
+        fc_view = fc_sum.rearrange("(b i p j) d -> b p i (j d)", i=FC_STEPS, p=P, j=SLOTS)
         out_view = out.rearrange("o (s p j) d -> s p o (j d)", p=P, j=SLOTS)
-        ch_view = child_h.rearrange("n k d -> (n k) d").rearrange(
-            "(b g q) d -> b q g d", g=BANK_GROUPS, q=P
-        )
+        ch_rows = child_h.rearrange("n k d -> (n k) d")
+        ch_view = ch_rows.rearrange("(s g q) d -> s q g d", g=SLOTS * BANK_GROUPS, q=P)
+        ch_wide_view = ch_rows.rearrange("(s g q r) d -> s q g (r d)", g=SLOTS * BANK_GROUPS // 2, q=P, r=2)
 
         x_sb, fc_sb, ch_sb, hT_ps, xT_ps = {}, {}, {}, {}, {}
         x_side, h_side, x_q, h_q, io_ps, u_ps = {}, {}, {}, {}, {}, {}
@@ -58,19 +61,25 @@ def tile_childsumtreelstmcell_pb_t_kernel(
         def load(s):
             if not live(s):
                 return
-            for b in range(SLOTS):
-                ch_sb[s, b] = loads.tile(
-                    [P, BANK_GROUPS, D], BF16, tag="ch", bufs=SLOTS * LOAD_AHEAD, name="ch_sb"
-                )
-                nc.sync.dma_start(out=ch_sb[s, b][:], in_=ch_view[SLOTS * s + b])
-            x_sb[s] = loads.tile([P, SLOTS * D], BF16, tag="x", name="x_sb")
-            nc.sync.dma_start(out=x_sb[s][:], in_=x_view[s])
+            ch_sb[s] = loads.tile([P, SLOTS * BANK_GROUPS, D], BF16, tag="ch", name="ch_sb")
+            if s in WIDE_STEPS:
+                wide = ch_sb[s][:].rearrange("q (g r) d -> q g (r d)", r=2)
+                nc.sync.dma_start(out=wide, in_=ch_wide_view[s])
+            elif s < 2:
+                for b in range(SLOTS):
+                    groups = slice(BANK_GROUPS * b, BANK_GROUPS * (b + 1))
+                    nc.sync.dma_start(out=ch_sb[s][:, groups], in_=ch_view[s][:, groups])
+            else:
+                nc.sync.dma_start(out=ch_sb[s][:], in_=ch_view[s])
+            if s % X_STEPS == 0:
+                x_sb[s] = loads.tile([P, X_STEPS, SLOTS * D], BF16, tag="x", bufs=5, name="x_sb")
+                nc.sync.dma_start(out=x_sb[s][:], in_=x_view[s // X_STEPS])
 
         def load_fc(s):
-            if not live(s):
+            if not live(s) or s % FC_STEPS != 0:
                 return
-            fc_sb[s] = loads.tile([P, SLOTS, H], BF16, tag="fc", name="fc_sb")
-            nc.sync.dma_start(out=fc_sb[s][:].rearrange("p j d -> p (j d)"), in_=fc_view[s])
+            fc_sb[s] = loads.tile([P, FC_STEPS, SLOTS * H], BF16, tag="fc", bufs=3, name="fc_sb")
+            nc.sync.dma_start(out=fc_sb[s][:], in_=fc_view[s // FC_STEPS])
 
         w_raw = const.tile([P, GATES, PACK, H], BF16)
         u_raw = const.tile([P, GATES, PACK, H], BF16)
@@ -109,15 +118,20 @@ def tile_childsumtreelstmcell_pb_t_kernel(
         warm = const.tile([P, 1], F32)
         nc.vector.memset(warm[:], 0.0)
         nc.scalar.activation(out=warm[:], in_=warm[:], func=ACT.Sigmoid)
-        sel_nat = const.tile([P, GROUP_NODES], F32)
-        nc.vector.tensor_reduce(
-            out=sel_nat[:],
-            in_=ident[:].rearrange("q (n k) -> q n k", k=CHILDREN),
-            axis=mybir.AxisListType.X,
-            op=ALU.add,
-        )
-        sel = const.tile([P, SLOTS, PG], BF16)
-        nc.vector.tensor_copy(out=sel[:], in_=sel_nat[:].rearrange("q (a j) -> q j a", j=SLOTS))
+        sel = {}
+        for rows in (1, 2):
+            nodes = rows * GROUP_NODES
+            sel_nat = const.tile([P, nodes], F32, name="sel_nat" + str(rows))
+            nc.vector.tensor_reduce(
+                out=sel_nat[:],
+                in_=ident[:].rearrange("q (n k) -> q n k", k=CHILDREN // rows),
+                axis=mybir.AxisListType.X,
+                op=ALU.add,
+            )
+            sel[rows] = const.tile([P, SLOTS, nodes // SLOTS], BF16, name="sel" + str(rows))
+            nc.vector.tensor_copy(
+                out=sel[rows][:], in_=sel_nat[:].rearrange("q (a j) -> q j a", j=SLOTS)
+            )
 
         bias = const.tile([P, GATES * H], F32)
 
@@ -148,15 +162,17 @@ def tile_childsumtreelstmcell_pb_t_kernel(
                 return
             for b in range(SLOTS):
                 hT_ps[s, b] = psum.tile([P, SLOTS, PACK, PB], F32, tag="hT", bufs=2 * SLOTS, name="hT_ps")
-                for g in range(BANK_GROUPS):
+                rows = 2 if s in WIDE_STEPS else 1
+                for g in range(BANK_GROUPS // rows):
                     for t in range(PACK):
-                        nc.tensor.matmul(
-                            out=hT_ps[s, b][:, :, t, PG * g : PG * (g + 1)],
-                            lhsT=ch_sb[s, b][:, g, t:D:PACK],
-                            rhs=sel[:],
-                            start=True,
-                            stop=True,
-                        )
+                        for r in range(rows):
+                            nc.tensor.matmul(
+                                out=hT_ps[s, b][:, :, t, rows * PG * g : rows * PG * (g + 1)],
+                                lhsT=ch_sb[s][:, BANK_GROUPS * b + rows * g + r, t:D:PACK],
+                                rhs=sel[rows][:],
+                                start=(r == 0),
+                                stop=(r == rows - 1),
+                            )
 
         def round_h(s):
             if not live(s):
@@ -173,7 +189,7 @@ def tile_childsumtreelstmcell_pb_t_kernel(
             if not live(s):
                 return
             xT_ps[s] = psum.tile([P, SLOTS, 2, P], F32, tag="xT", bufs=1, name="xT_ps")
-            words = x_sb[s][:].bitcast(F32)
+            words = x_sb[s - s % X_STEPS][:, s % X_STEPS].bitcast(F32)
             for j in range(SLOTS):
                 for u in range(2):
                     every_2nd = slice((D // 2) * j + u, (D // 2) * (j + 1), 2)
@@ -245,6 +261,9 @@ def tile_childsumtreelstmcell_pb_t_kernel(
                 gate = pre[s][:, :, lo : lo + H]
                 nc.scalar.activation(out=gate, in_=gate, func=func)
 
+        def fc_of(s):
+            return fc_sb[s - s % FC_STEPS][:, s % FC_STEPS].rearrange("p (j d) -> p j d", j=SLOTS)
+
         def new_out(s):
             out_sb[s] = work.tile([P, 2, SLOTS, H], F32, tag="out", bufs=STORE_LAG + 4, name="out_sb")
 
@@ -253,10 +272,11 @@ def tile_childsumtreelstmcell_pb_t_kernel(
                 return
             new_out(s)
             c_new = out_sb[s][:, 1]
-            nc.gpsimd.tensor_tensor(
+            engine = nc.vector if s == STEPS - 2 else nc.gpsimd
+            engine.tensor_tensor(
                 out=c_new, in0=pre[s][:, :, 0:H], in1=pre[s][:, :, 2 * H : 3 * H], op=ALU.mult
             )
-            nc.gpsimd.tensor_tensor(out=c_new, in0=c_new, in1=fc_sb[s][:], op=ALU.add)
+            engine.tensor_tensor(out=c_new, in0=c_new, in1=fc_of(s), op=ALU.add)
 
         def cell_last():
             s = STEPS - 1
@@ -267,7 +287,7 @@ def tile_childsumtreelstmcell_pb_t_kernel(
                     out=c_new[:, j], in0=pre[s][:, j, 0:H], in1=pre[s][:, j, 2 * H : 3 * H], op=ALU.mult
                 )
             for j in range(SLOTS):
-                nc.vector.tensor_tensor(out=c_new[:, j], in0=c_new[:, j], in1=fc_sb[s][:, j], op=ALU.add)
+                nc.vector.tensor_tensor(out=c_new[:, j], in0=c_new[:, j], in1=fc_of(s)[:, j], op=ALU.add)
 
         def finish_last():
             s = STEPS - 1
@@ -361,5 +381,10 @@ def tile_childsumtreelstmcell_pb_t_kernel(
         cell_last()
         hidden(STEPS - 2)
         finish_last()
-        for s in range(STEPS - 3 - STORE_LAG, STEPS):
+        for s in range(STEPS - 3 - STORE_LAG, STEPS - 2):
             store(s)
+        for s in (STEPS - 2, STEPS - 1):
+            for o in (1, 0):
+                nc.sync.dma_start(
+                    out=out_view[s][:, o], in_=out_sb[s][:, o].rearrange("p j d -> p (j d)")
+                )

@@ -58,9 +58,7 @@ def tile_childsumtreelstmcell_pb_t_kernel(
         def live(s):
             return 0 <= s < STEPS
 
-        def load(s):
-            if not live(s):
-                return
+        def load_children(s):
             ch_sb[s] = loads.tile([P, SLOTS * BANK_GROUPS, D], BF16, tag="ch", name="ch_sb")
             if s in WIDE_STEPS:
                 wide = ch_sb[s][:].rearrange("q (g r) d -> q g (r d)", r=2)
@@ -71,9 +69,16 @@ def tile_childsumtreelstmcell_pb_t_kernel(
                     nc.sync.dma_start(out=ch_sb[s][:, groups], in_=ch_view[s][:, groups])
             else:
                 nc.sync.dma_start(out=ch_sb[s][:], in_=ch_view[s])
+
+        def load_x(s):
             if s % X_STEPS == 0:
                 x_sb[s] = loads.tile([P, X_STEPS, SLOTS * D], BF16, tag="x", bufs=5, name="x_sb")
                 nc.sync.dma_start(out=x_sb[s][:], in_=x_view[s // X_STEPS])
+
+        def load(s):
+            if live(s):
+                load_children(s)
+                load_x(s)
 
         def load_fc(s):
             if not live(s) or s % FC_STEPS != 0:
@@ -110,9 +115,20 @@ def tile_childsumtreelstmcell_pb_t_kernel(
                 )
 
         bias_rows = const.tile([P, GATES * H], BF16)
-        nc.vector.memset(bias_rows[:], 0.0)
+        nc.vector.memset(bias_rows[:].bitcast(U32), 0)
+
+        def load_bias(g):
+            for row, vec in enumerate(((bWi, bUi), (bWo, bUo), (bWu, bUu))[g]):
+                nc.gpsimd.dma_start(
+                    out=bias_rows[row : row + 1, H * g : H * (g + 1)],
+                    in_=vec.rearrange("(o h) -> o h", o=1),
+                )
+
+        load_bias(0)
+        load_bias(1)
         ident = const.tile([P, P], F32)
         make_identity(nc, ident[:])
+        load_bias(2)
         ones = const.tile([P, P], BF16)
         nc.vector.memset(ones[:], 1.0)
         warm = const.tile([P, 1], F32)
@@ -135,14 +151,6 @@ def tile_childsumtreelstmcell_pb_t_kernel(
 
         bias = const.tile([P, GATES * H], F32)
 
-        def load_bias():
-            for g, (b_w, b_u) in enumerate(((bWi, bUi), (bWo, bUo), (bWu, bUu))):
-                cols = slice(H * g, H * (g + 1))
-                for row, vec in enumerate((b_w, b_u)):
-                    nc.gpsimd.dma_start(
-                        out=bias_rows[row : row + 1, cols], in_=vec.rearrange("(o h) -> o h", o=1)
-                    )
-
         def build_bias():
             bias_io_ps = psum.tile([P, 2 * H], F32, tag="hT", bufs=2 * SLOTS)
             nc.tensor.matmul(
@@ -154,8 +162,6 @@ def tile_childsumtreelstmcell_pb_t_kernel(
                 out=bias_u_ps[:], lhsT=ones[:], rhs=bias_rows[:, 2 * H : 3 * H], start=True, stop=True
             )
             nc.scalar.copy(out=bias[:, 2 * H : 3 * H], in_=bias_u_ps[:])
-
-        load_bias()
 
         def sum_children(s):
             if not live(s):
@@ -336,9 +342,10 @@ def tile_childsumtreelstmcell_pb_t_kernel(
             cell(t - 1)
             tanh_cell(t - 2)
 
+        load_children(0)
         load_gate(0)
         load_gate(1)
-        load(0)
+        load_x(0)
         load_gate(2)
         for t in range(1 - LOAD_AHEAD, 0):
             load(t + LOAD_AHEAD)
@@ -355,6 +362,7 @@ def tile_childsumtreelstmcell_pb_t_kernel(
         copy_x(0)
         arrange_w(2)
         arrange_u(2)
+        build_bias()
         quantise(0, h_side, h_q, "h")
         quantise(0, x_side, x_q, "x")
         quantise_gate(2)
@@ -363,7 +371,6 @@ def tile_childsumtreelstmcell_pb_t_kernel(
         multiply(0)
         sum_children(1)
         transpose_x(1)
-        build_bias()
         add_bias_io(0, 0)
         add_bias_io(0, 1)
         add_bias_u(0)

@@ -205,7 +205,7 @@ def tile_childsumtreelstmcell_pb_t_kernel(
             if not live(s):
                 return
             x_side[s] = sides.tile([P, SLOTS * P * PACK], BF16, align_bytes=64, tag="x_side", name="x_side")
-            nc.vector.tensor_copy(
+            nc.scalar.copy(
                 out=x_side[s][:].bitcast(F32).rearrange("w (j p u) -> w j p u", j=SLOTS, u=2),
                 in_=xT_ps[s][:].rearrange("w j u p -> w j p u"),
             )
@@ -282,7 +282,11 @@ def tile_childsumtreelstmcell_pb_t_kernel(
             engine.tensor_tensor(
                 out=c_new, in0=pre[s][:, :, 0:H], in1=pre[s][:, :, 2 * H : 3 * H], op=ALU.mult
             )
-            engine.tensor_tensor(out=c_new, in0=c_new, in1=fc_of(s), op=ALU.add)
+
+        def add_fc(s):
+            if live(s) and s < STEPS - 1:
+                c_new = out_sb[s][:, 1]
+                nc.vector.tensor_tensor(out=c_new, in0=c_new, in1=fc_of(s), op=ALU.add)
 
         def cell_last():
             s = STEPS - 1
@@ -328,6 +332,7 @@ def tile_childsumtreelstmcell_pb_t_kernel(
             load_fc(t + LOAD_AHEAD - FC_LATER)
             store(t - 3 - STORE_LAG)
             multiply(t)
+            add_fc(t - 2)
             hidden(t - 3)
             copy_x(t + 1)
             add_bias_io(t, 0)
@@ -382,6 +387,7 @@ def tile_childsumtreelstmcell_pb_t_kernel(
         quantise(1, x_side, x_q, "x")
         for t in range(1, STEPS):
             iteration(t)
+        add_fc(STEPS - 2)
         hidden(STEPS - 3)
         activate(STEPS - 1)
         tanh_cell(STEPS - 2)

from contextlib import ExitStack

import concourse.mybir as mybir
from concourse.masks import make_identity

F32 = mybir.dt.float32
BF16 = mybir.dt.bfloat16
U32 = mybir.dt.uint32
U8 = mybir.dt.uint8
FP8X4 = mybir.dt.float8_e4m3fn_x4
ACT = mybir.ActivationFunctionType
ALU = mybir.AluOpType

P = 128
PACK = 4
NODES, CHILDREN, D, H = 4096, 4, 512, 256
GATES = 3

SLOTS = 2
STEPS = NODES // (P * SLOTS)
GROUP_NODES = P // CHILDREN
BANK_GROUPS = 4
PG = GROUP_NODES // SLOTS
PB = PG * BANK_GROUPS
LOAD_AHEAD = 6
FC_LATER = 3
X_STEPS = 2
FC_STEPS = 4
WIDE_STEPS = (14, 15)
STORE_LAG = STEPS - LOAD_AHEAD - 3 + FC_LATER

FLOPS = 2 * NODES * D * H * 2 * GATES


def tile_childsumtreelstmcell_pb_t_kernel(
    tc, x, child_h, fc_sum, Wi, bWi, Ui, bUi, Wo, bWo, Uo, bUo, Wu, bWu, Uu, bUu, out
):
    nc = tc.nc
    with ExitStack() as ctx:
        ctx.enter_context(tc.manual_schedule())
        const = ctx.enter_context(tc.tile_pool(name="const", bufs=1))
        loads = ctx.enter_context(tc.tile_pool(name="loads", bufs=LOAD_AHEAD))
        sides = ctx.enter_context(tc.tile_pool(name="sides", bufs=2))
        work = ctx.enter_context(tc.tile_pool(name="work", bufs=2))
        psum = ctx.enter_context(tc.psum_pool(name="psum", bufs=1))

        x_view = x.rearrange("(b i p j) d -> b p i (j d)", i=X_STEPS, p=P, j=SLOTS)
        fc_view = fc_sum.rearrange("(b i p j) d -> b p i (j d)", i=FC_STEPS, p=P, j=SLOTS)
        out_view = out.rearrange("o (s p j) d -> s p o (j d)", p=P, j=SLOTS)
        ch_rows = child_h.rearrange("n k d -> (n k) d")
        ch_view = ch_rows.rearrange("(s g q) d -> s q g d", g=SLOTS * BANK_GROUPS, q=P)
        ch_wide_view = ch_rows.rearrange("(s g q r) d -> s q g (r d)", g=SLOTS * BANK_GROUPS // 2, q=P, r=2)

        x_sb, fc_sb, ch_sb, hT_ps, xT_ps = {}, {}, {}, {}, {}
        x_side, h_side, x_q, h_q, io_ps, u_ps = {}, {}, {}, {}, {}, {}
        pre, tanh_c, out_sb = {}, {}, {}

        def live(s):
            return 0 <= s < STEPS

        def load_children(s):
            ch_sb[s] = loads.tile([P, SLOTS * BANK_GROUPS, D], BF16, tag="ch", name="ch_sb")
            if s in WIDE_STEPS:
                wide = ch_sb[s][:].rearrange("q (g r) d -> q g (r d)", r=2)
                nc.sync.dma_start(out=wide, in_=ch_wide_view[s])
            elif s < 2:
                for b in range(SLOTS):
                    groups = slice(BANK_GROUPS * b, BANK_GROUPS * (b + 1))
                    nc.sync.dma_start(out=ch_sb[s][:, groups], in_=ch_view[s][:, groups])
            else:
                nc.sync.dma_start(out=ch_sb[s][:], in_=ch_view[s])

        def load_x(s):
            if s % X_STEPS == 0:
                x_sb[s] = loads.tile([P, X_STEPS, SLOTS * D], BF16, tag="x", bufs=5, name="x_sb")
                nc.sync.dma_start(out=x_sb[s][:], in_=x_view[s // X_STEPS])

        def load(s):
            if live(s):
                load_children(s)
                load_x(s)

        def load_fc(s):
            if not live(s) or s % FC_STEPS != 0:
                return
            fc_sb[s] = loads.tile([P, FC_STEPS, SLOTS * H], BF16, tag="fc", bufs=3, name="fc_sb")
            nc.sync.dma_start(out=fc_sb[s][:], in_=fc_view[s // FC_STEPS])

        w_raw = const.tile([P, GATES, PACK, H], BF16)
        u_raw = const.tile([P, GATES, PACK, H], BF16)
        w_side = const.tile([P, GATES, H, PACK], BF16, align_bytes=64)
        u_side = const.tile([P, GATES, H, PACK], BF16, align_bytes=64)
        w_codes = const.tile([P, GATES * H], U32, align_bytes=64)
        u_codes = const.tile([P, GATES * H], U32, align_bytes=64)
        w_scales = const.tile([P, GATES * H], U8, align_bytes=64)
        u_scales = const.tile([P, GATES * H], U8, align_bytes=64)

        def load_gate(g):
            for raw, mat in ((w_raw, (Wi, Wo, Wu)[g]), (u_raw, (Ui, Uo, Uu)[g])):
                nc.sync.dma_start(out=raw[:, g], in_=mat.rearrange("(w t) c -> w t c", t=PACK))

        def arrange_w(g):
            nc.vector.tensor_copy(out=w_side[:, g], in_=w_raw[:, g].rearrange("w t c -> w c t"))

        def arrange_u(g):
            nc.scalar.copy(out=u_side[:, g], in_=u_raw[:, g].rearrange("w t c -> w c t"))

        def quantise_gate(g):
            cols = slice(H * g, H * (g + 1))
            for side, codes, scales in ((w_side, w_codes, w_scales), (u_side, u_codes, u_scales)):
                nc.vector.quantize_mx(
                    out=codes[:, cols].bitcast(FP8X4),
                    scales=scales[:, cols],
                    in_=side[:, g].rearrange("w c t -> w (c t)"),
                )

        bias_rows = const.tile([P, GATES * H], BF16)
        nc.vector.memset(bias_rows[:].bitcast(U32), 0)

        def load_bias(g):
            for row, vec in enumerate(((bWi, bUi), (bWo, bUo), (bWu, bUu))[g]):
                nc.gpsimd.dma_start(
                    out=bias_rows[row : row + 1, H * g : H * (g + 1)],
                    in_=vec.rearrange("(o h) -> o h", o=1),
                )

        load_bias(0)
        load_bias(1)
        ident = const.tile([P, P], F32)
        make_identity(nc, ident[:])
        load_bias(2)
        ones = const.tile([P, P], BF16)
        nc.vector.memset(ones[:], 1.0)
        warm = const.tile([P, 1], F32)
        nc.vector.memset(warm[:], 0.0)
        nc.scalar.activation(out=warm[:], in_=warm[:], func=ACT.Sigmoid)
        sel = {}
        for rows in (1, 2):
            nodes = rows * GROUP_NODES
            sel_nat = const.tile([P, nodes], F32, name="sel_nat" + str(rows))
            nc.vector.tensor_reduce(
                out=sel_nat[:],
                in_=ident[:].rearrange("q (n k) -> q n k", k=CHILDREN // rows),
                axis=mybir.AxisListType.X,
                op=ALU.add,
            )
            sel[rows] = const.tile([P, SLOTS, nodes // SLOTS], BF16, name="sel" + str(rows))
            nc.vector.tensor_copy(
                out=sel[rows][:], in_=sel_nat[:].rearrange("q (a j) -> q j a", j=SLOTS)
            )

        bias = const.tile([P, GATES * H], F32)

        def build_bias():
            bias_io_ps = psum.tile([P, 2 * H], F32, tag="hT", bufs=2 * SLOTS)
            nc.tensor.matmul(
                out=bias_io_ps[:], lhsT=ones[:], rhs=bias_rows[:, 0 : 2 * H], start=True, stop=True
            )
            nc.scalar.copy(out=bias[:, 0 : 2 * H], in_=bias_io_ps[:])
            bias_u_ps = psum.tile([P, H], F32, tag="hT", bufs=2 * SLOTS)
            nc.tensor.matmul(
                out=bias_u_ps[:], lhsT=ones[:], rhs=bias_rows[:, 2 * H : 3 * H], start=True, stop=True
            )
            nc.scalar.copy(out=bias[:, 2 * H : 3 * H], in_=bias_u_ps[:])

        def sum_children(s):
            if not live(s):
                return
            for b in range(SLOTS):
                hT_ps[s, b] = psum.tile([P, SLOTS, PACK, PB], F32, tag="hT", bufs=2 * SLOTS, name="hT_ps")
                rows = 2 if s in WIDE_STEPS else 1
                for g in range(BANK_GROUPS // rows):
                    for t in range(PACK):
                        for r in range(rows):
                            nc.tensor.matmul(
                                out=hT_ps[s, b][:, :, t, rows * PG * g : rows * PG * (g + 1)],
                                lhsT=ch_sb[s][:, BANK_GROUPS * b + rows * g + r, t:D:PACK],
                                rhs=sel[rows][:],
                                start=(r == 0),
                                stop=(r == rows - 1),
                            )

        def round_h(s):
            if not live(s):
                return
            h_side[s] = sides.tile([P, SLOTS * P * PACK], BF16, align_bytes=64, tag="h_side", name="h_side")
            view = h_side[s][:].rearrange("w (j p t) -> w j p t", j=SLOTS, t=PACK)
            for b in range(SLOTS):
                nc.scalar.copy(
                    out=view[:, :, PB * b : PB * (b + 1), :],
                    in_=hT_ps[s, b][:].rearrange("w j t p -> w j p t"),
                )

        def transpose_x(s):
            if not live(s):
                return
            xT_ps[s] = psum.tile([P, SLOTS, 2, P], F32, tag="xT", bufs=1, name="xT_ps")
            words = x_sb[s - s % X_STEPS][:, s % X_STEPS].bitcast(F32)
            for j in range(SLOTS):
                for u in range(2):
                    every_2nd = slice((D // 2) * j + u, (D // 2) * (j + 1), 2)
                    nc.tensor.transpose(xT_ps[s][:, j, u, :], words[:, every_2nd], ident[:])

        def copy_x(s):
            if not live(s):
                return
            x_side[s] = sides.tile([P, SLOTS * P * PACK], BF16, align_bytes=64, tag="x_side", name="x_side")
            nc.scalar.copy(
                out=x_side[s][:].bitcast(F32).rearrange("w (j p u) -> w j p u", j=SLOTS, u=2),
                in_=xT_ps[s][:].rearrange("w j u p -> w j p u"),
            )

        def quantise(s, side, quantised, name):
            if not live(s):
                return
            codes = sides.tile([P, SLOTS * P], U32, align_bytes=64, tag=name + "_codes", name=name + "_codes")
            scales = sides.tile([P, SLOTS * P], U8, align_bytes=64, tag=name + "_scales", name=name + "_scales")
            nc.vector.quantize_mx(out=codes[:].bitcast(FP8X4), scales=scales[:], in_=side[s][:])
            quantised[s] = (codes, scales)

        def multiply(s):
            if not live(s):
                return
            for j in range(SLOTS):
                io_ps[s, j] = psum.tile([P, 2 * H], F32, tag="io", bufs=2, name="io_ps")
            u_ps[s] = psum.tile([P, SLOTS, H], F32, tag="u", bufs=1, name="u_ps")
            groups = [(io_ps[s, j][:], j, slice(0, 2 * H)) for j in range(SLOTS)]
            groups += [(u_ps[s][:, j, :], j, slice(2 * H, 3 * H)) for j in range(SLOTS)]
            for acc, j, cols in groups:
                nodes = slice(P * j, P * (j + 1))
                for part, (a_q, b_codes, b_scales) in enumerate(
                    ((x_q[s], w_codes, w_scales), (h_q[s], u_codes, u_scales))
                ):
                    nc.tensor.matmul_mx(
                        out=acc,
                        lhsT=a_q[0][:, nodes].bitcast(FP8X4),
                        lhsT_scale=a_q[1][:, nodes],
                        rhs=b_codes[:, cols].bitcast(FP8X4),
                        rhs_scale=b_scales[:, cols],
                        start=(part == 0),
                        stop=(part == 1),
                    )

        def add_bias_io(s, j):
            if not live(s):
                return
            if j == 0:
                pre[s] = work.tile([P, SLOTS, GATES * H], F32, tag="pre", bufs=4, name="pre")
            nc.vector.tensor_tensor(
                out=pre[s][:, j, 0 : 2 * H], in0=io_ps[s, j][:], in1=bias[:, 0 : 2 * H], op=ALU.add
            )

        def add_bias_u(s):
            if not live(s):
                return
            nc.vector.tensor_tensor(
                out=pre[s][:, :, 2 * H : 3 * H],
                in0=u_ps[s][:],
                in1=bias[:, 2 * H : 3 * H].unsqueeze(1).to_broadcast([P, SLOTS, H]),
                op=ALU.add,
            )

        def activate(s):
            if not live(s):
                return
            for lo, func in ((0, ACT.Sigmoid), (2 * H, ACT.Tanh), (H, ACT.Sigmoid)):
                gate = pre[s][:, :, lo : lo + H]
                nc.scalar.activation(out=gate, in_=gate, func=func)

        def fc_of(s):
            return fc_sb[s - s % FC_STEPS][:, s % FC_STEPS].rearrange("p (j d) -> p j d", j=SLOTS)

        def new_out(s):
            out_sb[s] = work.tile([P, 2, SLOTS, H], F32, tag="out", bufs=STORE_LAG + 4, name="out_sb")

        def cell(s):
            if not live(s):
                return
            new_out(s)
            c_new = out_sb[s][:, 1]
            engine = nc.vector if s == STEPS - 2 else nc.gpsimd
            engine.tensor_tensor(
                out=c_new, in0=pre[s][:, :, 0:H], in1=pre[s][:, :, 2 * H : 3 * H], op=ALU.mult
            )

        def add_fc(s):
            if live(s) and s < STEPS - 1:
                c_new = out_sb[s][:, 1]
                nc.vector.tensor_tensor(out=c_new, in0=c_new, in1=fc_of(s), op=ALU.add)

        def cell_last():
            s = STEPS - 1
            new_out(s)
            c_new = out_sb[s][:, 1]
            for j in range(SLOTS):
                nc.vector.tensor_tensor(
                    out=c_new[:, j], in0=pre[s][:, j, 0:H], in1=pre[s][:, j, 2 * H : 3 * H], op=ALU.mult
                )
            for j in range(SLOTS):
                nc.vector.tensor_tensor(out=c_new[:, j], in0=c_new[:, j], in1=fc_of(s)[:, j], op=ALU.add)

        def finish_last():
            s = STEPS - 1
            tanh_c[s] = work.tile([P, SLOTS, H], F32, tag="tanh_c", name="tanh_c")
            for j in range(SLOTS):
                nc.scalar.activation(out=tanh_c[s][:, j], in_=out_sb[s][:, 1, j], func=ACT.Tanh)
            for j in range(SLOTS):
                nc.vector.tensor_tensor(
                    out=out_sb[s][:, 0, j], in0=pre[s][:, j, H : 2 * H], in1=tanh_c[s][:, j], op=ALU.mult
                )

        def tanh_cell(s):
            if not live(s):
                return
            tanh_c[s] = work.tile([P, SLOTS, H], F32, tag="tanh_c", name="tanh_c")
            nc.scalar.activation(out=tanh_c[s][:], in_=out_sb[s][:, 1], func=ACT.Tanh)

        def hidden(s):
            if not live(s):
                return
            nc.vector.tensor_tensor(
                out=out_sb[s][:, 0], in0=pre[s][:, :, H : 2 * H], in1=tanh_c[s][:], op=ALU.mult
            )

        def store(s):
            if not live(s):
                return
            nc.sync.dma_start(out=out_view[s], in_=out_sb[s][:].rearrange("p o j d -> p o (j d)"))

        def iteration(t):
            load(t + LOAD_AHEAD)
            load_fc(t + LOAD_AHEAD - FC_LATER)
            store(t - 3 - STORE_LAG)
            multiply(t)
            add_fc(t - 2)
            hidden(t - 3)
            copy_x(t + 1)
            add_bias_io(t, 0)
            round_h(t + 1)
            quantise(t + 1, h_side, h_q, "h")
            quantise(t + 1, x_side, x_q, "x")
            add_bias_io(t, 1)
            add_bias_u(t)
            sum_children(t + 2)
            transpose_x(t + 2)
            activate(t - 1)
            cell(t - 1)
            tanh_cell(t - 2)

        load_children(0)
        load_gate(0)
        load_gate(1)
        load_x(0)
        load_gate(2)
        for t in range(1 - LOAD_AHEAD, 0):
            load(t + LOAD_AHEAD)
            load_fc(t + LOAD_AHEAD - FC_LATER)
        arrange_w(0)
        arrange_u(0)
        arrange_w(1)
        arrange_u(1)
        quantise_gate(0)
        quantise_gate(1)
        sum_children(0)
        transpose_x(0)
        round_h(0)
        copy_x(0)
        arrange_w(2)
        arrange_u(2)
        build_bias()
        quantise(0, h_side, h_q, "h")
        quantise(0, x_side, x_q, "x")
        quantise_gate(2)
        load(LOAD_AHEAD)
        load_fc(LOAD_AHEAD - FC_LATER)
        multiply(0)
        sum_children(1)
        transpose_x(1)
        add_bias_io(0, 0)
        add_bias_io(0, 1)
        add_bias_u(0)
        round_h(1)
        copy_x(1)
        sum_children(2)
        transpose_x(2)
        quantise(1, h_side, h_q, "h")
        quantise(1, x_side, x_q, "x")
        for t in range(1, STEPS):
            iteration(t)
        add_fc(STEPS - 2)
        hidden(STEPS - 3)
        activate(STEPS - 1)
        tanh_cell(STEPS - 2)
        cell_last()
        hidden(STEPS - 2)
        finish_last()
        for s in range(STEPS - 3 - STORE_LAG, STEPS - 2):
            store(s)
        for s in (STEPS - 2, STEPS - 1):
            for o in (1, 0):
                nc.sync.dma_start(
                    out=out_view[s][:, o], in_=out_sb[s][:, o].rearrange("p j d -> p (j d)")
                )
